import numpy as np
import ml_dtypes


def mxq(x, axis, fmt="e4m3"):
    dtype, down = {"e4m3": (ml_dtypes.float8_e4m3fn, 7), "e5m2": (ml_dtypes.float8_e5m2, 14)}[fmt]
    v = np.moveaxis(np.asarray(x, np.float32).astype(ml_dtypes.bfloat16).astype(np.float64), axis, -1)
    blocks = v.reshape(v.shape[:-1] + (-1, 32))
    amax = np.abs(blocks).max(-1, keepdims=True)
    byte = np.maximum(np.where(amax > 0, np.frexp(amax)[1] - 1 + 127, 0) - down, 1)
    scale = np.exp2(byte - 127.0)
    codes = (blocks / scale).astype(np.float32).astype(dtype).astype(np.float64)
    return np.moveaxis((codes * scale).reshape(v.shape), -1, axis)


WIDE = False


def mx_kscale(k):
    if not WIDE:
        return np.ones(k)
    levels = np.array([10, -10, 5, -5, 0])
    if k % 512:
        return np.exp2(np.random.permutation(np.resize(levels, k // 32))).repeat(32)
    a = np.empty((k // 512, 16))
    for p in range(k // 512):
        a[p, :8] = np.random.permutation(np.resize(levels, 8))
        for g in range(8):
            far = levels[np.abs(levels - a[p, g]) >= 10]
            a[p, g + 8] = far[np.random.randint(len(far))]
    return np.exp2(a.ravel()).repeat(32)


BF16 = ml_dtypes.bfloat16


def bf(x):
    return np.asarray(x, np.float32).astype(BF16)


def f64(x):
    return np.asarray(x).astype(np.float64)


B, N0, N1, N2, N3, T, K = 256, 512, 1024, 1024, 512, 8, 512
R = min(K, N0, N1)
R2 = min(R, T)
GS = 0.25


def setup_inputs():
    s, t = mx_kscale(R), mx_kscale(R)
    return {"S": bf(np.random.standard_normal((R, R, R2)) * s[:, None, None] * t[None, :, None]),
            "U0": bf(np.random.standard_normal((N1, R)) / np.sqrt(R) / s[None, :]),
            "U1": bf(np.random.standard_normal((N0, R)) * GS / np.sqrt(R) / t[None, :])}


def reference(S, U0, U1):
    w1 = f64(bf(mxq(f64(S).reshape(R, R * R2).T, 1, "e4m3") @ mxq(f64(U0).T, 0, "e4m3")))
    w2 = mxq(w1.reshape(R, R2 * N1).T, 1, "e4m3") @ mxq(f64(U1).T, 0, "e4m3")
    return w2.reshape(R2, N1, N0)

@@ -1,0 +1,196 @@
+from contextlib import ExitStack
+
+import concourse.masks as masks
+import concourse.mybir as mybir
+
+F32 = mybir.dt.float32
+BF16 = mybir.dt.bfloat16
+U32 = mybir.dt.uint32
+U8 = mybir.dt.uint8
+FP8X4 = mybir.dt.float8_e4m3fn_x4
+
+BANK_DT = BF16
+
+P = 128
+N_R = 8
+N_A = 8
+N_UNITS = 16
+FLOPS = 2 * 512 * 4096 * 1024 + 2 * 512 * 8192 * 512
+
+S_CHUNK_M = (32, 32, 32, 16, 16)
+
+
+def tile_mtl_net_tf_pa_kernel(tc, S, U0, U1, out):
+    nc = tc.nc
+    with ExitStack() as ctx:
+        keep = ctx.enter_context(tc.tile_pool(name="keep", bufs=1))
+        wpool = ctx.enter_context(tc.tile_pool(name="wpool", bufs=3))
+        opool = ctx.enter_context(tc.tile_pool(name="opool", bufs=4))
+        ps1 = ctx.enter_context(tc.psum_pool(name="ps1", bufs=4))
+        ps2 = ctx.enter_context(tc.psum_pool(name="ps2", bufs=4))
+
+        def copy_on(engine, dst, src):
+            if engine == "v":
+                nc.vector.tensor_copy(out=dst, in_=src)
+            else:
+                nc.scalar.copy(out=dst, in_=src)
+
+        u0_view = U0.rearrange("(m a) q -> m a q", a=N_A)
+        u0_raw = []
+        for h in range(2):
+            t_raw = keep.tile([P, 4, 512], BF16, name="u0_raw%d" % h)
+            nc.sync.dma_start(out=t_raw[:], in_=u0_view[:, 4 * h : 4 * h + 4, :])
+            u0_raw.append(t_raw)
+        s_view = S.rearrange("(k j) p r -> k j (p r)", j=4)
+        s_raw = []
+        u1_raw = keep.tile([P, 4, 512], BF16, name="u1_raw")
+        m0 = 0
+        for k, mc in enumerate(S_CHUNK_M):
+            t_raw = keep.tile([P, 4, 32 * mc], BF16, name="s_raw%d" % k)
+            nc.sync.dma_start(out=t_raw[:], in_=s_view[:, :, 32 * m0 : 32 * (m0 + mc)])
+            s_raw.append(t_raw)
+            m0 += mc
+        nc.sync.dma_start(out=u1_raw[:], in_=U1.rearrange("(b m) k -> m b k", b=4))
+
+        ident = keep.tile([P, P], F32, name="ident")
+        masks.make_identity(nc, ident[:])
+        warm_in = keep.tile([P, 8], F32, name="warm_in")
+        warm_out = keep.tile([P, 8], F32, name="warm_out")
+        nc.vector.memset(warm_in[:], 0.0)
+        nc.scalar.copy(out=warm_out[:], in_=warm_in[:])
+
+        def prepare_factor(raw, label):
+            words = raw[:].bitcast(F32)
+            grouped = keep.tile([P, 4, P, 4], BF16, name="grp_" + label, align_bytes=64)
+            grouped_words = grouped[:].bitcast(F32)
+            for pair in range(2):
+                xt = ps2.tile([P, 2, 2, P], F32, name="xt", tag="acc2")
+                for s in range(2):
+                    for u in range(2):
+                        nc.tensor.transpose(xt[:, s, u, :], words[:, 2 * pair + s, u:256:2], ident[:])
+                nc.scalar.copy(
+                    out=grouped_words[:, 2 * pair : 2 * pair + 2, :, :],
+                    in_=xt[:].rearrange("p s u m -> p s m u"),
+                )
+            codes = keep.tile([P, 512], U32, name="codes_" + label, align_bytes=64)
+            scales = keep.tile([P, 512], U8, name="scales_" + label, align_bytes=64)
+            nc.vector.quantize_mx(
+                out=codes[:].bitcast(FP8X4),
+                scales=scales[:],
+                in_=grouped[:].rearrange("p s m t -> p (s m t)"),
+            )
+            return codes, scales
+
+        u0_q = [prepare_factor(u0_raw[0], "u0a"), prepare_factor(u0_raw[1], "u0b")]
+
+        s_grp = [keep.tile([P, 4, 4, P, 4], BF16, name="s_grp%d" % rh, align_bytes=64) for rh in range(2)]
+        m0 = 0
+        for k, mc in enumerate(S_CHUNK_M):
+            src5 = s_raw[k][:].rearrange("p j (m t r) -> p j m t r", t=4, r=N_R)
+            for rh in range(2):
+                for t in range(4):
+                    engine = "s" if (t == 3 or (t == 2 and rh == 1 and k % 2 == 0)) else "v"
+                    copy_on(
+                        engine,
+                        s_grp[rh][:, :, t, m0 : m0 + mc, :].rearrange("p r m j -> p m r j"),
+                        src5[:, :, :, t, 4 * rh : 4 * rh + 4].rearrange("p j m r -> p m r j"),
+                    )
+            m0 += mc
+
+        s_q = {}
+
+        def quantize_s(r):
+            codes = keep.tile([P, 512], U32, name="s_codes%d" % r, align_bytes=64)
+            scales = keep.tile([P, 512], U8, name="s_scales%d" % r, align_bytes=64)
+            nc.vector.quantize_mx(
+                out=codes[:].bitcast(FP8X4),
+                scales=scales[:],
+                in_=s_grp[r // 4][:, r % 4, :, :, :].rearrange("p t m j -> p (t m j)"),
+            )
+            s_q[r] = (codes, scales)
+
+        w_bf = {}
+        w_q = {}
+        acc2 = {}
+        o_sb = {}
+
+        def stage1(u):
+            r, h = u // 2, u % 2
+            s_codes, s_scales = s_q[r]
+            f_codes, f_scales = u0_q[h]
+            w_bf[u] = wpool.tile([P, 4, P, 4], BF16, name="w_bf", tag="w_bf", align_bytes=64)
+            for g in range(4):
+                bank = ps1.tile([P, 4, P], BANK_DT, name="acc1", tag="acc1")
+                for t in range(4):
+                    nc.tensor.matmul_mx(
+                        out=bank[:, t, :],
+                        lhsT=s_codes[:, P * t : P * (t + 1)].bitcast(FP8X4),
+                        lhsT_scale=s_scales[:, P * t : P * (t + 1)],
+                        rhs=f_codes[:, P * g : P * (g + 1)].bitcast(FP8X4),
+                        rhs_scale=f_scales[:, P * g : P * (g + 1)],
+                        start=True,
+                        stop=True,
+                    )
+                engine = "v" if (u == 0 and g % 2 == 1) else "s"
+                copy_on(engine, w_bf[u][:, g, :, :], bank[:].rearrange("p t n -> p n t"))
+
+        def quantize_w(u):
+            codes = wpool.tile([P, 512], U32, name="w_codes", tag="w_codes", align_bytes=64)
+            scales = wpool.tile([P, 512], U8, name="w_scales", tag="w_scales", align_bytes=64)
+            nc.vector.quantize_mx(
+                out=codes[:].bitcast(FP8X4),
+                scales=scales[:],
+                in_=w_bf[u][:].rearrange("p g n t -> p (g n t)"),
+            )
+            w_q[u] = (codes, scales)
+
+        def stage2(u):
+            codes, scales = w_q[u]
+            u1_codes, u1_scales = u1_q[0]
+            o_sb[u] = opool.tile([P, 4, 512], F32, name="o_sb", tag="o_sb")
+            for g in range(4):
+                bank = ps2.tile([P, 512], F32, name="acc2", tag="acc2")
+                nc.tensor.matmul_mx(
+                    out=bank[:],
+                    lhsT=codes[:, P * g : P * (g + 1)].bitcast(FP8X4),
+                    lhsT_scale=scales[:, P * g : P * (g + 1)],
+                    rhs=u1_codes[:].bitcast(FP8X4),
+                    rhs_scale=u1_scales[:],
+                    start=True,
+                    stop=True,
+                )
+                acc2[(u, g)] = bank
+
+        def out_view(u):
+            r, h = u // 2, u % 2
+            return out[r].rearrange("(n a) i -> n a i", a=N_A)[:, 4 * h : 4 * h + 4, :]
+
+        def drain2(u, g):
+            if u >= N_UNITS - 2:
+                engine = "s" if g % 2 == 1 else "v"
+            else:
+                engine = "s" if (g == 3 and u % 4 != 3) else "v"
+            copy_on(engine, o_sb[u][:, g, :], acc2[(u, g)][:])
+            if u == N_UNITS - 1 and g >= 2:
+                nc.sync.dma_start(out=out_view(u)[:, g : g + 1, :], in_=o_sb[u][:, g : g + 1, :])
+            elif g % 2 == 1:
+                nc.sync.dma_start(out=out_view(u)[:, g - 1 : g + 1, :], in_=o_sb[u][:, g - 1 : g + 1, :])
+
+        u1_q = []
+        quantize_s(0)
+        stage1(0)
+        u1_q.append(prepare_factor(u1_raw, "u1"))
+        stage1(1)
+        quantize_s(1)
+        for u in range(N_UNITS):
+            quantize_w(u)
+            if u % 2 == 1 and (u + 3) // 2 < N_R:
+                quantize_s((u + 3) // 2)
+            if u > 0:
+                drain2(u - 1, 3)
+            stage2(u)
+            if u + 2 < N_UNITS:
+                stage1(u + 2)
+            for g in range(3):
+                drain2(u, g)
+        drain2(N_UNITS - 1, 3)

@@ -119,20 +119,24 @@ def tile_mtl_net_tf_pa_kernel(tc, S, U0, U1, out):
             s_codes, s_scales = s_q[r]
             f_codes, f_scales = u0_q[h]
             w_bf[u] = wpool.tile([P, 4, P, 4], BF16, name="w_bf", tag="w_bf", align_bytes=64)
-            for g in range(4):
-                bank = ps1.tile([P, 4, P], BANK_DT, name="acc1", tag="acc1")
+            for gp in range(2):
+                bank = ps1.tile([P, 4, 2 * P], BANK_DT, name="acc1", tag="acc1")
                 for t in range(4):
                     nc.tensor.matmul_mx(
                         out=bank[:, t, :],
                         lhsT=s_codes[:, P * t : P * (t + 1)].bitcast(FP8X4),
                         lhsT_scale=s_scales[:, P * t : P * (t + 1)],
-                        rhs=f_codes[:, P * g : P * (g + 1)].bitcast(FP8X4),
-                        rhs_scale=f_scales[:, P * g : P * (g + 1)],
+                        rhs=f_codes[:, 2 * P * gp : 2 * P * (gp + 1)].bitcast(FP8X4),
+                        rhs_scale=f_scales[:, 2 * P * gp : 2 * P * (gp + 1)],
                         start=True,
                         stop=True,
                     )
-                engine = "v" if (u == 0 and g % 2 == 1) else "s"
-                copy_on(engine, w_bf[u][:, g, :, :], bank[:].rearrange("p t n -> p n t"))
+                engine = "v" if (u == 0 and gp == 1) else "s"
+                copy_on(
+                    engine,
+                    w_bf[u][:, 2 * gp : 2 * gp + 2, :, :].rearrange("p g n t -> p (g n) t"),
+                    bank[:].rearrange("p t n -> p n t"),
+                )
 
         def quantize_w(u):
             codes = wpool.tile([P, 512], U32, name="w_codes", tag="w_codes", align_bytes=64)
@@ -169,7 +173,7 @@ def tile_mtl_net_tf_pa_kernel(tc, S, U0, U1, out):
             if u >= N_UNITS - 2:
                 engine = "s" if g % 2 == 1 else "v"
             else:
-                engine = "s" if (g == 3 and u % 4 != 3) else "v"
+                engine = "s" if (g == 3 and (u % 4 != 3 or u == 7)) else "v"
             copy_on(engine, o_sb[u][:, g, :], acc2[(u, g)][:])
             if u == N_UNITS - 1 and g >= 2:
                 nc.sync.dma_start(out=out_view(u)[:, g : g + 1, :], in_=o_sb[u][:, g : g + 1, :])

@@ -9,25 +9,28 @@ U32 = mybir.dt.uint32
 U8 = mybir.dt.uint8
 FP8X4 = mybir.dt.float8_e4m3fn_x4
 
-BANK_DT = BF16
-
 P = 128
 N_R = 8
 N_A = 8
-N_UNITS = 16
+N_GRAN = 32
 FLOPS = 2 * 512 * 4096 * 1024 + 2 * 512 * 8192 * 512
 
-S_CHUNK_M = (32, 32, 32, 16, 16)
+S_CHUNK_M = (16, 32, 32, 32, 16)
+U0_AFTER_CHUNK = 1
+WARM_MATMULS = 3
+LEAD1 = 3
+LEAD_R = 2
+LEAD_Q = 1
 
 
 def tile_mtl_net_tf_pa_kernel(tc, S, U0, U1, out):
     nc = tc.nc
     with ExitStack() as ctx:
         keep = ctx.enter_context(tc.tile_pool(name="keep", bufs=1))
-        wpool = ctx.enter_context(tc.tile_pool(name="wpool", bufs=3))
-        opool = ctx.enter_context(tc.tile_pool(name="opool", bufs=4))
-        ps1 = ctx.enter_context(tc.psum_pool(name="ps1", bufs=4))
-        ps2 = ctx.enter_context(tc.psum_pool(name="ps2", bufs=4))
+        wpool = ctx.enter_context(tc.tile_pool(name="wpool", bufs=4))
+        opool = ctx.enter_context(tc.tile_pool(name="opool", bufs=8))
+        ps1 = ctx.enter_context(tc.psum_pool(name="ps1", bufs=3))
+        ps2 = ctx.enter_context(tc.psum_pool(name="ps2", bufs=5))
 
         def copy_on(engine, dst, src):
             if engine == "v":
@@ -37,19 +40,22 @@ def tile_mtl_net_tf_pa_kernel(tc, S, U0, U1, out):
 
         u0_view = U0.rearrange("(m a) q -> m a q", a=N_A)
         u0_raw = []
-        for h in range(2):
-            t_raw = keep.tile([P, 4, 512], BF16, name="u0_raw%d" % h)
-            nc.sync.dma_start(out=t_raw[:], in_=u0_view[:, 4 * h : 4 * h + 4, :])
-            u0_raw.append(t_raw)
         s_view = S.rearrange("(k j) p r -> k j (p r)", j=4)
         s_raw = []
         u1_raw = keep.tile([P, 4, 512], BF16, name="u1_raw")
+        m_start = []
         m0 = 0
         for k, mc in enumerate(S_CHUNK_M):
             t_raw = keep.tile([P, 4, 32 * mc], BF16, name="s_raw%d" % k)
             nc.sync.dma_start(out=t_raw[:], in_=s_view[:, :, 32 * m0 : 32 * (m0 + mc)])
             s_raw.append(t_raw)
+            m_start.append(m0)
             m0 += mc
+            if k == U0_AFTER_CHUNK:
+                for h in range(2):
+                    t_raw = keep.tile([P, 4, 512], BF16, name="u0_raw%d" % h)
+                    nc.sync.dma_start(out=t_raw[:], in_=u0_view[:, 4 * h : 4 * h + 4, :])
+                    u0_raw.append(t_raw)
         nc.sync.dma_start(out=u1_raw[:], in_=U1.rearrange("(b m) k -> m b k", b=4))
 
         ident = keep.tile([P, P], F32, name="ident")
@@ -59,7 +65,7 @@ def tile_mtl_net_tf_pa_kernel(tc, S, U0, U1, out):
         nc.vector.memset(warm_in[:], 0.0)
         nc.scalar.copy(out=warm_out[:], in_=warm_in[:])
 
-        def prepare_factor(raw, label):
+        def transpose_factor(raw, label, engine):
             words = raw[:].bitcast(F32)
             grouped = keep.tile([P, 4, P, 4], BF16, name="grp_" + label, align_bytes=64)
             grouped_words = grouped[:].bitcast(F32)
@@ -68,10 +74,14 @@ def tile_mtl_net_tf_pa_kernel(tc, S, U0, U1, out):
                 for s in range(2):
                     for u in range(2):
                         nc.tensor.transpose(xt[:, s, u, :], words[:, 2 * pair + s, u:256:2], ident[:])
-                nc.scalar.copy(
-                    out=grouped_words[:, 2 * pair : 2 * pair + 2, :, :],
-                    in_=xt[:].rearrange("p s u m -> p s m u"),
+                copy_on(
+                    engine,
+                    grouped_words[:, 2 * pair : 2 * pair + 2, :, :],
+                    xt[:].rearrange("p s u m -> p s m u"),
                 )
+            return grouped
+
+        def quantize_factor(grouped, label):
             codes = keep.tile([P, 512], U32, name="codes_" + label, align_bytes=64)
             scales = keep.tile([P, 512], U8, name="scales_" + label, align_bytes=64)
             nc.vector.quantize_mx(
@@ -81,21 +91,16 @@ def tile_mtl_net_tf_pa_kernel(tc, S, U0, U1, out):
             )
             return codes, scales
 
-        u0_q = [prepare_factor(u0_raw[0], "u0a"), prepare_factor(u0_raw[1], "u0b")]
-
         s_grp = [keep.tile([P, 4, 4, P, 4], BF16, name="s_grp%d" % rh, align_bytes=64) for rh in range(2)]
-        m0 = 0
-        for k, mc in enumerate(S_CHUNK_M):
+
+        def copy_s(k, rh, t, engine):
+            mc = S_CHUNK_M[k]
             src5 = s_raw[k][:].rearrange("p j (m t r) -> p j m t r", t=4, r=N_R)
-            for rh in range(2):
-                for t in range(4):
-                    engine = "s" if (t == 3 or (t == 2 and rh == 1 and k % 2 == 0)) else "v"
-                    copy_on(
-                        engine,
-                        s_grp[rh][:, :, t, m0 : m0 + mc, :].rearrange("p r m j -> p m r j"),
-                        src5[:, :, :, t, 4 * rh : 4 * rh + 4].rearrange("p j m r -> p m r j"),
-                    )
-            m0 += mc
+            copy_on(
+                engine,
+                s_grp[rh][:, :, t, m_start[k] : m_start[k] + mc, :].rearrange("p r m j -> p m r j"),
+                src5[:, :, :, t, 4 * rh : 4 * rh + 4].rearrange("p j m r -> p m r j"),
+            )
 
         s_q = {}
 
@@ -109,92 +114,112 @@ def tile_mtl_net_tf_pa_kernel(tc, S, U0, U1, out):
             )
             s_q[r] = (codes, scales)
 
+        def warm_tensor_engine(k):
+            for i in range(WARM_MATMULS):
+                junk = ps2.tile([P, 512], F32, name="junk", tag="acc2")
+                nc.tensor.matmul(out=junk[:], lhsT=s_raw[k][:, i, 0:P], rhs=s_raw[k][:, i, 0:512], start=True, stop=True)
+
+        u0_grp = []
+        u0_q = []
+        last = len(S_CHUNK_M) - 1
+        for k in range(last):
+            for rh in range(2):
+                for t in range(4):
+                    copy_s(k, rh, t, "s" if (t == 3 or (t == 2 and rh == 1 and k % 2 == 0)) else "v")
+            if k == U0_AFTER_CHUNK:
+                u0_grp.append(transpose_factor(u0_raw[0], "u0a", "s"))
+                u0_grp.append(transpose_factor(u0_raw[1], "u0b", "s"))
+            if k == U0_AFTER_CHUNK + 1:
+                u0_q.append(quantize_factor(u0_grp[0], "u0a"))
+                u0_q.append(quantize_factor(u0_grp[1], "u0b"))
+            if k >= last - 2:
+                warm_tensor_engine(k)
+        for t in range(4):
+            copy_s(last, 0, t, "s" if t == 3 else "v")
+        quantize_s(0)
+        for t in range(4):
+            copy_s(last, 1, t, "s")
+
+        acc1 = {}
         w_bf = {}
         w_q = {}
         acc2 = {}
         o_sb = {}
 
-        def stage1(u):
-            r, h = u // 2, u % 2
+        def stage1(g):
+            r, c = g // 4, g % 4
             s_codes, s_scales = s_q[r]
-            f_codes, f_scales = u0_q[h]
-            w_bf[u] = wpool.tile([P, 4, P, 4], BF16, name="w_bf", tag="w_bf", align_bytes=64)
-            for gp in range(2):
-                bank = ps1.tile([P, 4, 2 * P], BANK_DT, name="acc1", tag="acc1")
-                for t in range(4):
-                    nc.tensor.matmul_mx(
-                        out=bank[:, t, :],
-                        lhsT=s_codes[:, P * t : P * (t + 1)].bitcast(FP8X4),
-                        lhsT_scale=s_scales[:, P * t : P * (t + 1)],
-                        rhs=f_codes[:, 2 * P * gp : 2 * P * (gp + 1)].bitcast(FP8X4),
-                        rhs_scale=f_scales[:, 2 * P * gp : 2 * P * (gp + 1)],
-                        start=True,
-                        stop=True,
-                    )
-                engine = "v" if (u == 0 and gp == 1) else "s"
-                copy_on(
-                    engine,
-                    w_bf[u][:, 2 * gp : 2 * gp + 2, :, :].rearrange("p g n t -> p (g n) t"),
-                    bank[:].rearrange("p t n -> p n t"),
+            f_codes, f_scales = u0_q[c // 2]
+            lo = 2 * P * (c % 2)
+            bank = ps1.tile([P, 4, 2 * P], BF16, name="acc1", tag="acc1")
+            for t in range(4):
+                nc.tensor.matmul_mx(
+                    out=bank[:, t, :],
+                    lhsT=s_codes[:, P * t : P * (t + 1)].bitcast(FP8X4),
+                    lhsT_scale=s_scales[:, P * t : P * (t + 1)],
+                    rhs=f_codes[:, lo : lo + 2 * P].bitcast(FP8X4),
+                    rhs_scale=f_scales[:, lo : lo + 2 * P],
+                    start=True,
+                    stop=True,
                 )
+            acc1[g] = bank
 
-        def quantize_w(u):
-            codes = wpool.tile([P, 512], U32, name="w_codes", tag="w_codes", align_bytes=64)
-            scales = wpool.tile([P, 512], U8, name="w_scales", tag="w_scales", align_bytes=64)
+        def read1(g, engine):
+            w_bf[g] = wpool.tile([P, 2 * P, 4], BF16, name="w_bf", tag="w_bf", align_bytes=64)
+            copy_on(engine, w_bf[g][:], acc1[g][:].rearrange("p t n -> p n t"))
+
+        def quantize_w(g):
+            codes = wpool.tile([P, 2 * P], U32, name="w_codes", tag="w_codes", align_bytes=64)
+            scales = wpool.tile([P, 2 * P], U8, name="w_scales", tag="w_scales", align_bytes=64)
             nc.vector.quantize_mx(
                 out=codes[:].bitcast(FP8X4),
                 scales=scales[:],
-                in_=w_bf[u][:].rearrange("p g n t -> p (g n t)"),
+                in_=w_bf[g][:].rearrange("p n t -> p (n t)"),
             )
-            w_q[u] = (codes, scales)
+            w_q[g] = (codes, scales)
 
-        def stage2(u):
-            codes, scales = w_q[u]
+        def stage2(g):
+            codes, scales = w_q[g]
             u1_codes, u1_scales = u1_q[0]
-            o_sb[u] = opool.tile([P, 4, 512], F32, name="o_sb", tag="o_sb")
-            for g in range(4):
+            for e in range(2):
                 bank = ps2.tile([P, 512], F32, name="acc2", tag="acc2")
                 nc.tensor.matmul_mx(
                     out=bank[:],
-                    lhsT=codes[:, P * g : P * (g + 1)].bitcast(FP8X4),
-                    lhsT_scale=scales[:, P * g : P * (g + 1)],
+                    lhsT=codes[:, P * e : P * (e + 1)].bitcast(FP8X4),
+                    lhsT_scale=scales[:, P * e : P * (e + 1)],
                     rhs=u1_codes[:].bitcast(FP8X4),
                     rhs_scale=u1_scales[:],
                     start=True,
                     stop=True,
                 )
-                acc2[(u, g)] = bank
+                acc2[(g, e)] = bank
 
-        def out_view(u):
-            r, h = u // 2, u % 2
-            return out[r].rearrange("(n a) i -> n a i", a=N_A)[:, 4 * h : 4 * h + 4, :]
-
-        def drain2(u, g):
-            if u >= N_UNITS - 2:
-                engine = "s" if g % 2 == 1 else "v"
-            else:
-                engine = "s" if (g == 3 and (u % 4 != 3 or u == 7)) else "v"
-            copy_on(engine, o_sb[u][:, g, :], acc2[(u, g)][:])
-            if u == N_UNITS - 1 and g >= 2:
-                nc.sync.dma_start(out=out_view(u)[:, g : g + 1, :], in_=o_sb[u][:, g : g + 1, :])
-            elif g % 2 == 1:
-                nc.sync.dma_start(out=out_view(u)[:, g - 1 : g + 1, :], in_=o_sb[u][:, g - 1 : g + 1, :])
+        def read2(g, engines):
+            r, c = g // 4, g % 4
+            dst = out[r].rearrange("(n a) i -> n a i", a=N_A)
+            o_sb[g] = opool.tile([P, 2, 512], F32, name="o_sb", tag="o_sb")
+            for e in range(2):
+                copy_on(engines[e], o_sb[g][:, e, :], acc2[(g, e)][:])
+                if g == N_GRAN - 1:
+                    nc.sync.dma_start(out=dst[:, 2 * c + e : 2 * c + e + 1, :], in_=o_sb[g][:, e : e + 1, :])
+            if g < N_GRAN - 1:
+                nc.sync.dma_start(out=dst[:, 2 * c : 2 * c + 2, :], in_=o_sb[g][:])
 
         u1_q = []
-        quantize_s(0)
         stage1(0)
-        u1_q.append(prepare_factor(u1_raw, "u1"))
-        stage1(1)
         quantize_s(1)
-        for u in range(N_UNITS):
-            quantize_w(u)
-            if u % 2 == 1 and (u + 3) // 2 < N_R:
-                quantize_s((u + 3) // 2)
-            if u > 0:
-                drain2(u - 1, 3)
-            stage2(u)
-            if u + 2 < N_UNITS:
-                stage1(u + 2)
-            for g in range(3):
-                drain2(u, g)
-        drain2(N_UNITS - 1, 3)
+        u1_grp = transpose_factor(u1_raw, "u1", "v")
+        u1_q.append(quantize_factor(u1_grp, "u1"))
+        for k in range(1 - LEAD1, N_GRAN + 1):
+            if 0 < k + LEAD1 < N_GRAN:
+                stage1(k + LEAD1)
+            if 0 <= k + LEAD_R < N_GRAN:
+                read1(k + LEAD_R, "s")
+            if k > 0 and k % 4 == 3 and (k + 5) // 4 < N_R:
+                quantize_s((k + 5) // 4)
+            if 0 <= k + LEAD_Q < N_GRAN:
+                quantize_w(k + LEAD_Q)
+            if 0 <= k < N_GRAN:
+                stage2(k)
+            if 0 <= k - 1:
+                read2(k - 1, ("v", "s" if (k % 3 == 1 or k + LEAD_R >= N_GRAN) else "v"))

@@ -18,9 +18,9 @@ FLOPS = 2 * 512 * 4096 * 1024 + 2 * 512 * 8192 * 512
 S_CHUNK_M = (16, 32, 32, 32, 16)
 U0_AFTER_CHUNK = 1
 WARM_MATMULS = 3
-LEAD1 = 3
-LEAD_R = 2
-LEAD_Q = 1
+LEAD1 = 4
+LEAD_R = 3
+LEAD_Q = 2
 
 
 def tile_mtl_net_tf_pa_kernel(tc, S, U0, U1, out):
@@ -104,15 +104,16 @@ def tile_mtl_net_tf_pa_kernel(tc, S, U0, U1, out):
 
         s_q = {}
 
-        def quantize_s(r):
-            codes = keep.tile([P, 512], U32, name="s_codes%d" % r, align_bytes=64)
-            scales = keep.tile([P, 512], U8, name="s_scales%d" % r, align_bytes=64)
+        def quantize_s(r, count):
+            codes = keep.tile([P, count, 512], U32, name="s_codes%d" % r, align_bytes=64)
+            scales = keep.tile([P, count, 512], U8, name="s_scales%d" % r, align_bytes=64)
             nc.vector.quantize_mx(
-                out=codes[:].bitcast(FP8X4),
-                scales=scales[:],
-                in_=s_grp[r // 4][:, r % 4, :, :, :].rearrange("p t m j -> p (t m j)"),
+                out=codes[:].rearrange("p c w -> p (c w)").bitcast(FP8X4),
+                scales=scales[:].rearrange("p c w -> p (c w)"),
+                in_=s_grp[r // 4][:, r % 4 : r % 4 + count, :, :, :].rearrange("p c t m j -> p (c t m j)"),
             )
-            s_q[r] = (codes, scales)
+            for i in range(count):
+                s_q[r + i] = (codes[:, i, :], scales[:, i, :])
 
         def warm_tensor_engine(k):
             for i in range(WARM_MATMULS):
@@ -136,7 +137,7 @@ def tile_mtl_net_tf_pa_kernel(tc, S, U0, U1, out):
                 warm_tensor_engine(k)
         for t in range(4):
             copy_s(last, 0, t, "s" if t == 3 else "v")
-        quantize_s(0)
+        quantize_s(0, 1)
         for t in range(4):
             copy_s(last, 1, t, "s")
 
@@ -165,28 +166,31 @@ def tile_mtl_net_tf_pa_kernel(tc, S, U0, U1, out):
             acc1[g] = bank
 
         def read1(g, engine):
-            w_bf[g] = wpool.tile([P, 2 * P, 4], BF16, name="w_bf", tag="w_bf", align_bytes=64)
-            copy_on(engine, w_bf[g][:], acc1[g][:].rearrange("p t n -> p n t"))
+            if g % 2 == 0:
+                w_bf[g // 2] = wpool.tile([P, 4 * P, 4], BF16, name="w_bf", tag="w_bf", align_bytes=64)
+            lo = 2 * P * (g % 2)
+            copy_on(engine, w_bf[g // 2][:, lo : lo + 2 * P, :], acc1[g][:].rearrange("p t n -> p n t"))
 
-        def quantize_w(g):
-            codes = wpool.tile([P, 2 * P], U32, name="w_codes", tag="w_codes", align_bytes=64)
-            scales = wpool.tile([P, 2 * P], U8, name="w_scales", tag="w_scales", align_bytes=64)
+        def quantize_w(u):
+            codes = wpool.tile([P, 4 * P], U32, name="w_codes", tag="w_codes", align_bytes=64)
+            scales = wpool.tile([P, 4 * P], U8, name="w_scales", tag="w_scales", align_bytes=64)
             nc.vector.quantize_mx(
                 out=codes[:].bitcast(FP8X4),
                 scales=scales[:],
-                in_=w_bf[g][:].rearrange("p n t -> p (n t)"),
+                in_=w_bf[u][:].rearrange("p n t -> p (n t)"),
             )
-            w_q[g] = (codes, scales)
+            w_q[u] = (codes, scales)
 
         def stage2(g):
-            codes, scales = w_q[g]
+            codes, scales = w_q[g // 2]
             u1_codes, u1_scales = u1_q[0]
             for e in range(2):
                 bank = ps2.tile([P, 512], F32, name="acc2", tag="acc2")
+                lo = P * (2 * (g % 2) + e)
                 nc.tensor.matmul_mx(
                     out=bank[:],
-                    lhsT=codes[:, P * e : P * (e + 1)].bitcast(FP8X4),
-                    lhsT_scale=scales[:, P * e : P * (e + 1)],
+                    lhsT=codes[:, lo : lo + P].bitcast(FP8X4),
+                    lhsT_scale=scales[:, lo : lo + P],
                     rhs=u1_codes[:].bitcast(FP8X4),
                     rhs_scale=u1_scales[:],
                     start=True,
@@ -207,7 +211,7 @@ def tile_mtl_net_tf_pa_kernel(tc, S, U0, U1, out):
 
         u1_q = []
         stage1(0)
-        quantize_s(1)
+        quantize_s(1, 1)
         u1_grp = transpose_factor(u1_raw, "u1", "v")
         u1_q.append(quantize_factor(u1_grp, "u1"))
         for k in range(1 - LEAD1, N_GRAN + 1):
@@ -215,10 +219,10 @@ def tile_mtl_net_tf_pa_kernel(tc, S, U0, U1, out):
                 stage1(k + LEAD1)
             if 0 <= k + LEAD_R < N_GRAN:
                 read1(k + LEAD_R, "s")
-            if k > 0 and k % 4 == 3 and (k + 5) // 4 < N_R:
-                quantize_s((k + 5) // 4)
-            if 0 <= k + LEAD_Q < N_GRAN:
-                quantize_w(k + LEAD_Q)
+            if k > 0 and k % 8 == 2 and (k + 6) // 4 < N_R:
+                quantize_s((k + 6) // 4, 2)
+            if 0 <= k + LEAD_Q < N_GRAN and (k + LEAD_Q) % 2 == 1:
+                quantize_w((k + LEAD_Q) // 2)
             if 0 <= k < N_GRAN:
                 stage2(k)
             if 0 <= k - 1:

@@ -15,7 +15,7 @@ N_A = 8
 N_GRAN = 32
 FLOPS = 2 * 512 * 4096 * 1024 + 2 * 512 * 8192 * 512
 
-S_CHUNK_M = (16, 32, 32, 32, 16)
+S_CHUNK_M = (16, 48, 48, 16)
 U0_AFTER_CHUNK = 1
 WARM_MATMULS = 3
 LEAD1 = 4
@@ -137,6 +137,7 @@ def tile_mtl_net_tf_pa_kernel(tc, S, U0, U1, out):
                 warm_tensor_engine(k)
         for t in range(4):
             copy_s(last, 0, t, "s" if t == 3 else "v")
+        warm_tensor_engine(last)
         quantize_s(0, 1)
         for t in range(4):
             copy_s(last, 1, t, "s")
@@ -202,11 +203,15 @@ def tile_mtl_net_tf_pa_kernel(tc, S, U0, U1, out):
             r, c = g // 4, g % 4
             dst = out[r].rearrange("(n a) i -> n a i", a=N_A)
             o_sb[g] = opool.tile([P, 2, 512], F32, name="o_sb", tag="o_sb")
-            for e in range(2):
-                copy_on(engines[e], o_sb[g][:, e, :], acc2[(g, e)][:])
-                if g == N_GRAN - 1:
-                    nc.sync.dma_start(out=dst[:, 2 * c + e : 2 * c + e + 1, :], in_=o_sb[g][:, e : e + 1, :])
-            if g < N_GRAN - 1:
+            pieces = 2 if g == N_GRAN - 1 else 1
+            width = 512 // pieces
+            for i in range(pieces):
+                cols = slice(width * i, width * (i + 1))
+                for e in range(2):
+                    copy_on(engines[e], o_sb[g][:, e, cols], acc2[(g, e)][:, cols])
+                    if g >= N_GRAN - 2:
+                        nc.sync.dma_start(out=dst[:, 2 * c + e : 2 * c + e + 1, cols], in_=o_sb[g][:, e : e + 1, cols])
+            if g < N_GRAN - 2:
                 nc.sync.dma_start(out=dst[:, 2 * c : 2 * c + 2, :], in_=o_sb[g][:])
 
         u1_q = []
@@ -226,4 +231,4 @@ def tile_mtl_net_tf_pa_kernel(tc, S, U0, U1, out):
             if 0 <= k < N_GRAN:
                 stage2(k)
             if 0 <= k - 1:
-                read2(k - 1, ("v", "s" if (k % 3 == 1 or k + LEAD_R >= N_GRAN) else "v"))
+                read2(k - 1, ("v", "s" if (k % 3 == 1 or k + LEAD_R > N_GRAN) else "v"))

@@ -137,7 +137,6 @@ def tile_mtl_net_tf_pa_kernel(tc, S, U0, U1, out):
                 warm_tensor_engine(k)
         for t in range(4):
             copy_s(last, 0, t, "s" if t == 3 else "v")
-        warm_tensor_engine(last)
         quantize_s(0, 1)
         for t in range(4):
             copy_s(last, 1, t, "s")
@@ -203,15 +202,11 @@ def tile_mtl_net_tf_pa_kernel(tc, S, U0, U1, out):
             r, c = g // 4, g % 4
             dst = out[r].rearrange("(n a) i -> n a i", a=N_A)
             o_sb[g] = opool.tile([P, 2, 512], F32, name="o_sb", tag="o_sb")
-            pieces = 2 if g == N_GRAN - 1 else 1
-            width = 512 // pieces
-            for i in range(pieces):
-                cols = slice(width * i, width * (i + 1))
-                for e in range(2):
-                    copy_on(engines[e], o_sb[g][:, e, cols], acc2[(g, e)][:, cols])
-                    if g >= N_GRAN - 2:
-                        nc.sync.dma_start(out=dst[:, 2 * c + e : 2 * c + e + 1, cols], in_=o_sb[g][:, e : e + 1, cols])
-            if g < N_GRAN - 2:
+            for e in range(2):
+                copy_on(engines[e], o_sb[g][:, e, :], acc2[(g, e)][:])
+                if g == N_GRAN - 1:
+                    nc.sync.dma_start(out=dst[:, 2 * c + e : 2 * c + e + 1, :], in_=o_sb[g][:, e : e + 1, :])
+            if g < N_GRAN - 1:
                 nc.sync.dma_start(out=dst[:, 2 * c : 2 * c + 2, :], in_=o_sb[g][:])
 
         u1_q = []

from contextlib import ExitStack

import concourse.masks as masks
import concourse.mybir as mybir

F32 = mybir.dt.float32
BF16 = mybir.dt.bfloat16
U32 = mybir.dt.uint32
U8 = mybir.dt.uint8
FP8X4 = mybir.dt.float8_e4m3fn_x4

P = 128
N_R = 8
N_A = 8
N_GRAN = 32
FLOPS = 2 * 512 * 4096 * 1024 + 2 * 512 * 8192 * 512

S_CHUNK_M = (16, 48, 48, 16)
U0_AFTER_CHUNK = 1
WARM_MATMULS = 3
LEAD1 = 4
LEAD_R = 3
LEAD_Q = 2


def tile_mtl_net_tf_pa_kernel(tc, S, U0, U1, out):
    nc = tc.nc
    with ExitStack() as ctx:
        keep = ctx.enter_context(tc.tile_pool(name="keep", bufs=1))
        wpool = ctx.enter_context(tc.tile_pool(name="wpool", bufs=4))
        opool = ctx.enter_context(tc.tile_pool(name="opool", bufs=8))
        ps1 = ctx.enter_context(tc.psum_pool(name="ps1", bufs=3))
        ps2 = ctx.enter_context(tc.psum_pool(name="ps2", bufs=5))

        def copy_on(engine, dst, src):
            if engine == "v":
                nc.vector.tensor_copy(out=dst, in_=src)
            else:
                nc.scalar.copy(out=dst, in_=src)

        u0_view = U0.rearrange("(m a) q -> m a q", a=N_A)
        u0_raw = []
        s_view = S.rearrange("(k j) p r -> k j (p r)", j=4)
        s_raw = []
        u1_raw = keep.tile([P, 4, 512], BF16, name="u1_raw")
        m_start = []
        m0 = 0
        for k, mc in enumerate(S_CHUNK_M):
            t_raw = keep.tile([P, 4, 32 * mc], BF16, name="s_raw%d" % k)
            nc.sync.dma_start(out=t_raw[:], in_=s_view[:, :, 32 * m0 : 32 * (m0 + mc)])
            s_raw.append(t_raw)
            m_start.append(m0)
            m0 += mc
            if k == U0_AFTER_CHUNK:
                for h in range(2):
                    t_raw = keep.tile([P, 4, 512], BF16, name="u0_raw%d" % h)
                    nc.sync.dma_start(out=t_raw[:], in_=u0_view[:, 4 * h : 4 * h + 4, :])
                    u0_raw.append(t_raw)
        nc.sync.dma_start(out=u1_raw[:], in_=U1.rearrange("(b m) k -> m b k", b=4))

        ident = keep.tile([P, P], F32, name="ident")
        masks.make_identity(nc, ident[:])
        warm_in = keep.tile([P, 8], F32, name="warm_in")
        warm_out = keep.tile([P, 8], F32, name="warm_out")
        nc.vector.memset(warm_in[:], 0.0)
        nc.scalar.copy(out=warm_out[:], in_=warm_in[:])

        def transpose_factor(raw, label, engine):
            words = raw[:].bitcast(F32)
            grouped = keep.tile([P, 4, P, 4], BF16, name="grp_" + label, align_bytes=64)
            grouped_words = grouped[:].bitcast(F32)
            for pair in range(2):
                xt = ps2.tile([P, 2, 2, P], F32, name="xt", tag="acc2")
                for s in range(2):
                    for u in range(2):
                        nc.tensor.transpose(xt[:, s, u, :], words[:, 2 * pair + s, u:256:2], ident[:])
                copy_on(
                    engine,
                    grouped_words[:, 2 * pair : 2 * pair + 2, :, :],
                    xt[:].rearrange("p s u m -> p s m u"),
                )
            return grouped

        def quantize_factor(grouped, label):
            codes = keep.tile([P, 512], U32, name="codes_" + label, align_bytes=64)
            scales = keep.tile([P, 512], U8, name="scales_" + label, align_bytes=64)
            nc.vector.quantize_mx(
                out=codes[:].bitcast(FP8X4),
                scales=scales[:],
                in_=grouped[:].rearrange("p s m t -> p (s m t)"),
            )
            return codes, scales

        s_grp = [keep.tile([P, 4, 4, P, 4], BF16, name="s_grp%d" % rh, align_bytes=64) for rh in range(2)]

        def copy_s(k, rh, t, engine):
            mc = S_CHUNK_M[k]
            src5 = s_raw[k][:].rearrange("p j (m t r) -> p j m t r", t=4, r=N_R)
            copy_on(
                engine,
                s_grp[rh][:, :, t, m_start[k] : m_start[k] + mc, :].rearrange("p r m j -> p m r j"),
                src5[:, :, :, t, 4 * rh : 4 * rh + 4].rearrange("p j m r -> p m r j"),
            )

        s_q = {}

        def quantize_s(r, count):
            codes = keep.tile([P, count, 512], U32, name="s_codes%d" % r, align_bytes=64)
            scales = keep.tile([P, count, 512], U8, name="s_scales%d" % r, align_bytes=64)
            nc.vector.quantize_mx(
                out=codes[:].rearrange("p c w -> p (c w)").bitcast(FP8X4),
                scales=scales[:].rearrange("p c w -> p (c w)"),
                in_=s_grp[r // 4][:, r % 4 : r % 4 + count, :, :, :].rearrange("p c t m j -> p (c t m j)"),
            )
            for i in range(count):
                s_q[r + i] = (codes[:, i, :], scales[:, i, :])

        def warm_tensor_engine(k):
            for i in range(WARM_MATMULS):
                junk = ps2.tile([P, 512], F32, name="junk", tag="acc2")
                nc.tensor.matmul(out=junk[:], lhsT=s_raw[k][:, i, 0:P], rhs=s_raw[k][:, i, 0:512], start=True, stop=True)

        u0_grp = []
        u0_q = []
        last = len(S_CHUNK_M) - 1
        for k in range(last):
            for rh in range(2):
                for t in range(4):
                    copy_s(k, rh, t, "s" if (t == 3 or (t == 2 and rh == 1 and k % 2 == 0)) else "v")
            if k == U0_AFTER_CHUNK:
                u0_grp.append(transpose_factor(u0_raw[0], "u0a", "s"))
                u0_grp.append(transpose_factor(u0_raw[1], "u0b", "s"))
            if k == U0_AFTER_CHUNK + 1:
                u0_q.append(quantize_factor(u0_grp[0], "u0a"))
                u0_q.append(quantize_factor(u0_grp[1], "u0b"))
            if k >= last - 2:
                warm_tensor_engine(k)
        for t in range(4):
            copy_s(last, 0, t, "s" if t == 3 else "v")
        quantize_s(0, 1)
        for t in range(4):
            copy_s(last, 1, t, "s")

        acc1 = {}
        w_bf = {}
        w_q = {}
        acc2 = {}
        o_sb = {}

        def stage1(g):
            r, c = g // 4, g % 4
            s_codes, s_scales = s_q[r]
            f_codes, f_scales = u0_q[c // 2]
            lo = 2 * P * (c % 2)
            bank = ps1.tile([P, 4, 2 * P], BF16, name="acc1", tag="acc1")
            for t in range(4):
                nc.tensor.matmul_mx(
                    out=bank[:, t, :],
                    lhsT=s_codes[:, P * t : P * (t + 1)].bitcast(FP8X4),
                    lhsT_scale=s_scales[:, P * t : P * (t + 1)],
                    rhs=f_codes[:, lo : lo + 2 * P].bitcast(FP8X4),
                    rhs_scale=f_scales[:, lo : lo + 2 * P],
                    start=True,
                    stop=True,
                )
            acc1[g] = bank

        def read1(g, engine):
            if g % 2 == 0:
                w_bf[g // 2] = wpool.tile([P, 4 * P, 4], BF16, name="w_bf", tag="w_bf", align_bytes=64)
            lo = 2 * P * (g % 2)
            copy_on(engine, w_bf[g // 2][:, lo : lo + 2 * P, :], acc1[g][:].rearrange("p t n -> p n t"))

        def quantize_w(u):
            codes = wpool.tile([P, 4 * P], U32, name="w_codes", tag="w_codes", align_bytes=64)
            scales = wpool.tile([P, 4 * P], U8, name="w_scales", tag="w_scales", align_bytes=64)
            nc.vector.quantize_mx(
                out=codes[:].bitcast(FP8X4),
                scales=scales[:],
                in_=w_bf[u][:].rearrange("p n t -> p (n t)"),
            )
            w_q[u] = (codes, scales)

        def stage2(g):
            codes, scales = w_q[g // 2]
            u1_codes, u1_scales = u1_q[0]
            for e in range(2):
                bank = ps2.tile([P, 512], F32, name="acc2", tag="acc2")
                lo = P * (2 * (g % 2) + e)
                nc.tensor.matmul_mx(
                    out=bank[:],
                    lhsT=codes[:, lo : lo + P].bitcast(FP8X4),
                    lhsT_scale=scales[:, lo : lo + P],
                    rhs=u1_codes[:].bitcast(FP8X4),
                    rhs_scale=u1_scales[:],
                    start=True,
                    stop=True,
                )
                acc2[(g, e)] = bank

        def read2(g, engines):
            r, c = g // 4, g % 4
            dst = out[r].rearrange("(n a) i -> n a i", a=N_A)
            o_sb[g] = opool.tile([P, 2, 512], F32, name="o_sb", tag="o_sb")
            for e in range(2):
                copy_on(engines[e], o_sb[g][:, e, :], acc2[(g, e)][:])
                if g == N_GRAN - 1:
                    nc.sync.dma_start(out=dst[:, 2 * c + e : 2 * c + e + 1, :], in_=o_sb[g][:, e : e + 1, :])
            if g < N_GRAN - 1:
                nc.sync.dma_start(out=dst[:, 2 * c : 2 * c + 2, :], in_=o_sb[g][:])

        u1_q = []
        stage1(0)
        quantize_s(1, 1)
        u1_grp = transpose_factor(u1_raw, "u1", "v")
        u1_q.append(quantize_factor(u1_grp, "u1"))
        for k in range(1 - LEAD1, N_GRAN + 1):
            if 0 < k + LEAD1 < N_GRAN:
                stage1(k + LEAD1)
            if 0 <= k + LEAD_R < N_GRAN:
                read1(k + LEAD_R, "s")
            if k > 0 and k % 8 == 2 and (k + 6) // 4 < N_R:
                quantize_s((k + 6) // 4, 2)
            if 0 <= k + LEAD_Q < N_GRAN and (k + LEAD_Q) % 2 == 1:
                quantize_w((k + LEAD_Q) // 2)
            if 0 <= k < N_GRAN:
                stage2(k)
            if 0 <= k - 1:
                read2(k - 1, ("v", "s" if (k % 3 == 1 or k + LEAD_R > N_GRAN) else "v"))
